import numpy as np
import ml_dtypes


def mxq(x, axis, fmt="e4m3"):
    dtype, down = {"e4m3": (ml_dtypes.float8_e4m3fn, 7), "e5m2": (ml_dtypes.float8_e5m2, 14)}[fmt]
    v = np.moveaxis(np.asarray(x, np.float32).astype(ml_dtypes.bfloat16).astype(np.float64), axis, -1)
    blocks = v.reshape(v.shape[:-1] + (-1, 32))
    amax = np.abs(blocks).max(-1, keepdims=True)
    byte = np.maximum(np.where(amax > 0, np.frexp(amax)[1] - 1 + 127, 0) - down, 1)
    scale = np.exp2(byte - 127.0)
    codes = (blocks / scale).astype(np.float32).astype(dtype).astype(np.float64)
    return np.moveaxis((codes * scale).reshape(v.shape), -1, axis)


WIDE = False


def mx_kscale(k):
    if not WIDE:
        return np.ones(k)
    levels = np.array([10, -10, 5, -5, 0])
    a = np.random.permutation(np.resize(levels, k // 512 * 4)).reshape(k // 512, 4)
    idx = np.arange(k)
    return np.exp2(a[idx // 512, idx % 128 // 32])


BF16 = ml_dtypes.bfloat16


def bf(x):
    return np.asarray(x, np.float32).astype(BF16)


def f64(x):
    return np.asarray(x).astype(np.float64)


E2M1 = np.array([0.0, 0.5, 1.0, 1.5, 2.0, 3.0, 4.0, 6.0, -0.0, -0.5, -1.0, -1.5, -2.0, -3.0, -4.0, -6.0])


def pack_weight(w, fmt):
    k, n = w.shape
    w = f64(bf(w)).reshape(k // 32, 32, n)
    amax = np.abs(w).max(1)
    if fmt == "e4m3":
        byte = np.frexp(amax)[1] - 1 + 127 - 7
    else:
        mant, ex = np.frexp(amax / 6.0)
        byte = np.where(mant > 0.5, ex, ex - 1) + 127
    byte = np.clip(np.where(amax > 0, byte, 1), 1, 254)
    scaled = (w * np.exp2(127.0 - byte)[:, None, :]).reshape(k, n).astype(np.float32)
    by_word = np.ascontiguousarray(scaled.reshape(k // 512, 128, 4, n).transpose(0, 1, 3, 2))
    if fmt == "e4m3":
        words = by_word.astype(ml_dtypes.float8_e4m3fn).view(np.uint8)
    else:
        c = by_word.astype(ml_dtypes.float4_e2m1fn).view(np.uint8) & 0xF
        words = c[..., 0::2] | (c[..., 1::2] << 4)
    return np.ascontiguousarray(words), np.ascontiguousarray(byte.astype(np.uint8).reshape(k // 512, 16, n))


def unpack_weight(words, scales, fmt):
    g, p, n, _ = words.shape
    if fmt == "e4m3":
        vals = np.ascontiguousarray(words).view(ml_dtypes.float8_e4m3fn).astype(np.float64)
    else:
        nib = np.empty((g, p, n, 4), np.uint8)
        nib[..., 0::2] = words & 0xF
        nib[..., 1::2] = words >> 4
        vals = E2M1[nib]
    vals = vals * np.repeat(np.exp2(scales.astype(np.float64) - 127.0), 8, axis=1)[..., None]
    return vals.transpose(0, 1, 3, 2).reshape(g * 512, n)


B, C, D, H, W, W0, W1 = 2, 512, 128, 32, 32, 64, 256
N = H * W
FMT = "e4m3"


def setup_inputs():
    s = mx_kscale(C)
    x = bf(np.random.standard_normal((B, C, N)))
    out1 = bf(np.random.standard_normal((B, C, N)) * 0.6 * s[None, :, None])
    q = bf(np.random.standard_normal((B, N, D)) * 0.42)
    k = bf(np.random.standard_normal((B, D, N)) * 0.42)
    wv2 = np.random.standard_normal((C, C)) * 4.0 / np.sqrt(C) / s[None, :]
    wv2_words, wv2_scales = pack_weight(np.ascontiguousarray(wv2.T), FMT)
    bv2 = bf(np.random.standard_normal(C) * 0.3)
    gamma = bf(1.0 + 0.1 * np.random.standard_normal(1))
    return {
        "x": x,
        "out1": out1,
        "q": q,
        "k": k,
        "wv2_words": wv2_words,
        "wv2_scales": wv2_scales,
        "bv2": bv2,
        "gamma": gamma,
    }


def reference(x, out1, q, k, wv2_words, wv2_scales, bv2, gamma):
    val = (unpack_weight(wv2_words, wv2_scales, FMT).T @ mxq(f64(out1), 1, "e4m3")) + f64(bv2)[None, :, None]
    s = f64(q) @ f64(k)
    e = np.exp(s - s.max(-1, keepdims=True))
    out = (mxq(val, 2, "e4m3") @ mxq(e, 2, "e4m3").transpose(0, 2, 1)) / e.sum(-1)[:, None, :]
    return f64(gamma)[0] * out + f64(x)

@@ -1,0 +1,329 @@
+from contextlib import ExitStack
+
+import concourse.mybir as mybir
+from concourse.masks import make_identity
+
+F32 = mybir.dt.float32
+BF16 = mybir.dt.bfloat16
+I32 = mybir.dt.int32
+U32 = mybir.dt.uint32
+U8 = mybir.dt.uint8
+FP8X4 = mybir.dt.float8_e4m3fn_x4
+ALU = mybir.AluOpType
+ACT = mybir.ActivationFunctionType
+AXIS_X = mybir.AxisListType.X
+
+P = 128
+PACK = 4
+K_PASS = P * PACK
+BANK = 512
+
+B, C, D, N = 2, 512, 128, 1024
+KEY_PASSES = N // K_PASS
+C_TILES = C // P
+M_TILES = N // P
+TILES = B * M_TILES
+CHUNKS = KEY_PASSES * C_TILES
+
+FLOPS = B * (2 * C * C * N + 2 * N * N * D + 2 * C * N * N)
+
+
+def tile_mvpam_module_mask_cascade_pb_kernel(
+    tc, x, out1, q, k, wv2_words, wv2_scales, bv2, gamma, out
+):
+    nc = tc.nc
+    with ExitStack() as ctx:
+        const = ctx.enter_context(tc.tile_pool(name="const", bufs=1))
+        batch = ctx.enter_context(tc.tile_pool(name="batch", bufs=1))
+        stream = ctx.enter_context(tc.tile_pool(name="stream", bufs=2))
+        stats = ctx.enter_context(tc.tile_pool(name="stats", bufs=3))
+        ps_scores = ctx.enter_context(tc.psum_pool(name="ps_scores", bufs=2))
+        ps_flip = ctx.enter_context(tc.psum_pool(name="ps_flip", bufs=1))
+        ps_work = ctx.enter_context(tc.psum_pool(name="ps_work", bufs=3))
+        ctx.enter_context(tc.manual_schedule())
+
+        k_sb, q_sb, qT, x_sb = {}, {}, {}, {}
+        f_raw, f_grp, f_codes, f_scales = {}, {}, {}, {}
+        v_grp, v_codes, v_scales = {}, {}, {}
+        for b in range(B):
+            k_sb[b] = batch.tile([P, N], BF16, name="k_sb%d" % b)
+            q_sb[b] = batch.tile([P, M_TILES, D], BF16, name="q_sb%d" % b)
+            qT[b] = batch.tile([P, N], BF16, name="qT%d" % b)
+            x_sb[b] = batch.tile([P, C_TILES, N], BF16, name="x_sb%d" % b)
+            f_raw[b] = batch.tile([P, PACK, N], BF16, name="f_raw%d" % b)
+            f_grp[b] = batch.tile(
+                [P, KEY_PASSES, PACK, P, PACK], BF16, name="f_grp%d" % b, align_bytes=64
+            )
+            f_codes[b] = batch.tile([P, N], U32, name="f_codes%d" % b, align_bytes=64)
+            f_scales[b] = batch.tile([P, N], U8, name="f_scales%d" % b, align_bytes=64)
+            v_grp[b] = batch.tile(
+                [P, KEY_PASSES, C, PACK], BF16, name="v_grp%d" % b, align_bytes=64
+            )
+            v_codes[b] = batch.tile([P, KEY_PASSES, C], U32, name="v_codes%d" % b, align_bytes=64)
+            v_scales[b] = batch.tile([P, KEY_PASSES, C], U8, name="v_scales%d" % b, align_bytes=64)
+
+        w_codes = const.tile([P, C], U32, name="w_codes", align_bytes=64)
+        w_scales = const.tile([P, C], U8, name="w_scales", align_bytes=64)
+        ident_bf = const.tile([P, P], BF16, name="ident_bf")
+        ident_f32 = const.tile([P, P], F32, name="ident_f32")
+        ones_bf = const.tile([P, P], BF16, name="ones_bf")
+        bias_row = const.tile([P, C], BF16, name="bias_row")
+        bias_all = const.tile([P, C], F32, name="bias_all")
+        gamma_bf = const.tile([P, 1], BF16, name="gamma_bf")
+        gamma_f32 = const.tile([P, 1], F32, name="gamma_f32")
+
+        nc.vector.memset(w_scales[:].bitcast(I32), 0)
+        nc.vector.memset(bias_row[:], 0.0)
+        nc.vector.memset(ones_bf[:], 1.0)
+        make_identity(nc, ident_bf[:])
+        make_identity(nc, ident_f32[:])
+
+        def load_scores_operands(b):
+            nc.sync.dma_start(out=k_sb[b][:], in_=k[b])
+            nc.sync.dma_start(
+                out=q_sb[b][:], in_=q[b].rearrange("(p i) d -> p i d", i=M_TILES)
+            )
+
+        def load_features(b):
+            nc.sync.dma_start(
+                out=f_raw[b][:], in_=out1[b].rearrange("(p j) n -> p j n", j=PACK)
+            )
+
+        load_scores_operands(0)
+        load_features(0)
+        nc.sync.dma_start(
+            out=w_codes[:].bitcast(I32),
+            in_=wv2_words[0].rearrange("p n t -> p (n t)").bitcast(I32),
+        )
+        for quad in range(4):
+            nc.sync.dma_start(
+                out=w_scales[32 * quad : 32 * quad + 4, :].bitcast(I32),
+                in_=wv2_scales[0, 4 * quad : 4 * quad + 4, :].bitcast(I32),
+            )
+        nc.gpsimd.dma_start(out=bias_row[0:1, :], in_=bv2.unsqueeze(0))
+        nc.gpsimd.dma_start(out=gamma_bf[:], in_=gamma.partition_broadcast(P))
+        load_scores_operands(1)
+        load_features(1)
+        for b in range(B):
+            nc.sync.dma_start(out=x_sb[b][:], in_=x[b].rearrange("(t p) m -> p t m", p=P))
+
+        def prepare_queries(b, copy):
+            flipped = ps_work.tile([P, M_TILES, P], BF16, name="qT_ps", tag="work")
+            for i in range(M_TILES):
+                nc.tensor.transpose(flipped[:, i, :], q_sb[b][:, i, :], ident_bf[:])
+            copy(
+                out=qT[b][:].rearrange("d (p i) -> d p i", i=M_TILES),
+                in_=flipped[:].rearrange("d i p -> d p i"),
+            )
+
+        def group_features(b, g, copy):
+            copy(
+                out=f_grp[b][:, g],
+                in_=f_raw[b][:, :, g * K_PASS : (g + 1) * K_PASS].rearrange(
+                    "p j (r t) -> p t r j", t=PACK
+                ),
+            )
+
+        def quantise_features(b, g):
+            cols = slice(g * K_PASS, (g + 1) * K_PASS)
+            nc.vector.quantize_mx(
+                out=f_codes[b][:, cols].bitcast(FP8X4),
+                scales=f_scales[b][:, cols],
+                in_=f_grp[b][:, g].rearrange("p t r j -> p (t r j)"),
+            )
+
+        val_ps = {}
+
+        def multiply_values(b, chunk):
+            g, ct = divmod(chunk, C_TILES)
+            if ct == 0:
+                quantise_features(b, g)
+            channels = slice(ct * P, (ct + 1) * P)
+            val_ps[b, chunk] = ps_work.tile([P, PACK, P], F32, name="val_ps", tag="work")
+            for t in range(PACK):
+                keys = slice((g * PACK + t) * P, (g * PACK + t + 1) * P)
+                nc.tensor.matmul_mx(
+                    out=val_ps[b, chunk][:, t, :],
+                    lhsT=f_codes[b][:, keys].bitcast(FP8X4),
+                    lhsT_scale=f_scales[b][:, keys],
+                    rhs=w_codes[:, channels].bitcast(FP8X4),
+                    rhs_scale=w_scales[:, channels],
+                    start=True,
+                    stop=True,
+                )
+
+        def round_values(b, chunk):
+            g, ct = divmod(chunk, C_TILES)
+            channels = slice(ct * P, (ct + 1) * P)
+            nc.vector.tensor_tensor(
+                out=v_grp[b][:, g, channels, :],
+                in0=val_ps[b, chunk][:].rearrange("p t c -> p c t"),
+                in1=bias_all[:, channels].unsqueeze(2).to_broadcast([P, P, PACK]),
+                op=ALU.add,
+            )
+            if ct == C_TILES - 1:
+                nc.vector.quantize_mx(
+                    out=v_codes[b][:, g, :].bitcast(FP8X4),
+                    scales=v_scales[b][:, g, :],
+                    in_=v_grp[b][:, g].rearrange("p c t -> p (c t)"),
+                )
+
+        s_ps, neg_max, e_sb, e_sums, e_grp, e_codes, e_scales = {}, {}, {}, {}, {}, {}, {}
+        eT_ps, inv_sum, acc, o_sb, oT_ps = {}, {}, {}, {}, {}
+
+        def scores(i):
+            b, mt = divmod(i, M_TILES)
+            s_ps[i] = ps_scores.tile([P, KEY_PASSES, BANK], F32, name="s_ps")
+            for g in range(KEY_PASSES):
+                nc.tensor.matmul(
+                    out=s_ps[i][:, g, :],
+                    lhsT=qT[b][:, mt * P : (mt + 1) * P],
+                    rhs=k_sb[b][:, g * BANK : (g + 1) * BANK],
+                    start=True,
+                    stop=True,
+                )
+
+        def row_max(i):
+            bank_max = stats.tile([P, KEY_PASSES], F32, name="bank_max")
+            for g in range(KEY_PASSES):
+                nc.vector.reduce_max(out=bank_max[:, g : g + 1], in_=s_ps[i][:, g, :], axis=AXIS_X)
+            neg_max[i] = stats.tile([P, 1], F32, name="neg_max")
+            nc.vector.tensor_reduce(
+                out=neg_max[i][:], in_=bank_max[:], axis=AXIS_X, op=ALU.max, negate=True
+            )
+
+        def exponentials(i):
+            e_sb[i] = stream.tile([P, N], BF16, name="e_sb")
+            e_sums[i] = stats.tile([P, KEY_PASSES], F32, name="e_sums")
+            for g in range(KEY_PASSES):
+                nc.scalar.activation(
+                    out=e_sb[i][:, g * K_PASS : (g + 1) * K_PASS].rearrange(
+                        "m (u r e) -> m u r e", u=2, e=2
+                    ),
+                    in_=s_ps[i][:, g, :].rearrange("m (r u e) -> m u r e", u=2, e=2),
+                    func=ACT.Exp,
+                    bias=neg_max[i][:, 0:1],
+                    scale=1.0,
+                    accum_out=e_sums[i][:, g : g + 1],
+                )
+
+        def flip_e(i):
+            words = e_sb[i][:].bitcast(F32)
+            eT_ps[i] = ps_flip.tile([P, 2 * KEY_PASSES, P], F32, name="eT_ps")
+            for gu in range(2 * KEY_PASSES):
+                nc.tensor.transpose(
+                    eT_ps[i][:, gu, :], words[:, gu * P : (gu + 1) * P], ident_f32[:]
+                )
+
+        def gather_e(i):
+            e_grp[i] = stream.tile([P, N], BF16, name="e_grp", align_bytes=64)
+            nc.scalar.copy(
+                out=e_grp[i][:].bitcast(F32).rearrange("r (g m u) -> r g m u", g=KEY_PASSES, u=2),
+                in_=eT_ps[i][:].rearrange("r (g u) m -> r g m u", g=KEY_PASSES),
+            )
+
+        def quantise_e(i):
+            e_codes[i] = stream.tile([P, KEY_PASSES * P], U32, name="e_codes", align_bytes=64)
+            e_scales[i] = stream.tile([P, KEY_PASSES * P], U8, name="e_scales", align_bytes=64)
+            nc.vector.quantize_mx(
+                out=e_codes[i][:].bitcast(FP8X4), scales=e_scales[i][:], in_=e_grp[i][:]
+            )
+            total = stats.tile([P, 1], F32, name="total")
+            nc.vector.reduce_sum(out=total[:], in_=e_sums[i][:], axis=AXIS_X)
+            inv_sum[i] = stats.tile([P, 1], F32, name="inv_sum")
+            nc.vector.reciprocal(out=inv_sum[i][:], in_=total[:])
+
+        def attend(i):
+            b = i // M_TILES
+            acc[i] = ps_work.tile([P, C], F32, name="acc", tag="work")
+            for g in range(KEY_PASSES):
+                queries = slice(g * P, (g + 1) * P)
+                nc.tensor.matmul_mx(
+                    out=acc[i][:],
+                    lhsT=e_codes[i][:, queries].bitcast(FP8X4),
+                    lhsT_scale=e_scales[i][:, queries],
+                    rhs=v_codes[b][:, g, :].bitcast(FP8X4),
+                    rhs_scale=v_scales[b][:, g, :],
+                    start=(g == 0),
+                    stop=(g == KEY_PASSES - 1),
+                )
+
+        def normalise(i):
+            o_sb[i] = stream.tile([P, C], F32, name="o_sb")
+            nc.scalar.activation(out=o_sb[i][:], in_=acc[i][:], func=ACT.Copy, scale=inv_sum[i][:, 0:1])
+
+        def flip_back(i):
+            oT_ps[i] = ps_work.tile([P, C_TILES, P], F32, name="oT_ps", tag="work")
+            for ct in range(C_TILES):
+                nc.tensor.transpose(
+                    oT_ps[i][:, ct, :], o_sb[i][:, ct * P : (ct + 1) * P], ident_f32[:]
+                )
+
+        def finish(i):
+            b, mt = divmod(i, M_TILES)
+            queries = slice(mt * P, (mt + 1) * P)
+            result = stream.tile([P, C_TILES, P], F32, name="result", bufs=3)
+            nc.vector.scalar_tensor_tensor(
+                out=result[:],
+                in0=oT_ps[i][:],
+                scalar=gamma_f32[:, 0:1],
+                in1=x_sb[b][:, :, queries],
+                op0=ALU.mult,
+                op1=ALU.add,
+            )
+            nc.sync.dma_start(
+                out=out[b].rearrange("(t p) m -> p t m", p=P)[:, :, queries], in_=result[:]
+            )
+
+        prepare_queries(0, nc.vector.tensor_copy)
+        scores(0)
+        bias_ps = ps_work.tile([P, C], F32, name="bias_ps", tag="work")
+        nc.tensor.matmul(out=bias_ps[:], lhsT=ones_bf[:], rhs=bias_row[:], start=True, stop=True)
+        nc.scalar.copy(out=bias_all[:], in_=bias_ps[:])
+        nc.vector.tensor_copy(out=gamma_f32[:], in_=gamma_bf[:])
+        row_max(0)
+        group_features(0, 0, nc.vector.tensor_copy)
+        group_features(0, 1, nc.scalar.copy)
+
+        def live(i):
+            return 0 <= i < TILES
+
+        def chunk_of_step(step):
+            before, chunk = divmod(step - 1, M_TILES)
+            return before + 1, chunk
+
+        for step in range(TILES + 3):
+            upcoming, chunk = chunk_of_step(step - 1)
+            if 1 <= upcoming < B:
+                round_values(upcoming, chunk)
+            if live(step - 3):
+                normalise(step - 3)
+            if live(step + 1):
+                scores(step + 1)
+            if live(step - 2):
+                quantise_e(step - 2)
+            if live(step):
+                exponentials(step)
+            if live(step - 1):
+                flip_e(step - 1)
+            if live(step - 3):
+                flip_back(step - 3)
+            if live(step + 1):
+                row_max(step + 1)
+            if live(step - 1):
+                gather_e(step - 1)
+            if live(step - 2):
+                attend(step - 2)
+            if live(step - 3):
+                finish(step - 3)
+            if step == 0:
+                for chunk in range(CHUNKS):
+                    multiply_values(0, chunk)
+                    round_values(0, chunk)
+            upcoming, chunk = chunk_of_step(step)
+            if 1 <= upcoming < B:
+                multiply_values(upcoming, chunk)
+            if step % M_TILES == 0 and step // M_TILES + 1 < B:
+                prepare_queries(step // M_TILES + 1, nc.scalar.copy)
+                for g in range(KEY_PASSES):
+                    group_features(step // M_TILES + 1, g, nc.scalar.copy)

@@ -84,13 +84,15 @@ def tile_mvpam_module_mask_cascade_pb_kernel(
                 out=q_sb[b][:], in_=q[b].rearrange("(p i) d -> p i d", i=M_TILES)
             )
 
-        def load_features(b):
+        def load_features(b, g):
+            keys = slice(g * K_PASS, (g + 1) * K_PASS)
             nc.sync.dma_start(
-                out=f_raw[b][:], in_=out1[b].rearrange("(p j) n -> p j n", j=PACK)
+                out=f_raw[b][:, :, keys],
+                in_=out1[b].rearrange("(p j) n -> p j n", j=PACK)[:, :, keys],
             )
 
         load_scores_operands(0)
-        load_features(0)
+        load_features(0, 0)
         nc.sync.dma_start(
             out=w_codes[:].bitcast(I32),
             in_=wv2_words[0].rearrange("p n t -> p (n t)").bitcast(I32),
@@ -100,10 +102,12 @@ def tile_mvpam_module_mask_cascade_pb_kernel(
                 out=w_scales[32 * quad : 32 * quad + 4, :].bitcast(I32),
                 in_=wv2_scales[0, 4 * quad : 4 * quad + 4, :].bitcast(I32),
             )
-        nc.gpsimd.dma_start(out=bias_row[0:1, :], in_=bv2.unsqueeze(0))
-        nc.gpsimd.dma_start(out=gamma_bf[:], in_=gamma.partition_broadcast(P))
+        nc.sync.dma_start(out=bias_row[0:1, :], in_=bv2.unsqueeze(0))
+        load_features(0, 1)
         load_scores_operands(1)
-        load_features(1)
+        load_features(1, 0)
+        load_features(1, 1)
+        nc.sync.dma_start(out=gamma_bf[:], in_=gamma.partition_broadcast(P))
         for b in range(B):
             nc.sync.dma_start(out=x_sb[b][:], in_=x[b].rearrange("(t p) m -> p t m", p=P))
 
@@ -134,16 +138,19 @@ def tile_mvpam_module_mask_cascade_pb_kernel(
 
         val_ps = {}
 
-        def multiply_values(b, chunk):
-            g, ct = divmod(chunk, C_TILES)
-            if ct == 0:
-                quantise_features(b, g)
+        def place_of_chunk(v):
+            b, rest = divmod(v, CHUNKS)
+            g, ct = divmod(rest, C_TILES)
+            return b, g, ct
+
+        def multiply_values(v):
+            b, g, ct = place_of_chunk(v)
             channels = slice(ct * P, (ct + 1) * P)
-            val_ps[b, chunk] = ps_work.tile([P, PACK, P], F32, name="val_ps", tag="work")
+            val_ps[v] = ps_work.tile([P, PACK, P], F32, name="val_ps", tag="work")
             for t in range(PACK):
                 keys = slice((g * PACK + t) * P, (g * PACK + t + 1) * P)
                 nc.tensor.matmul_mx(
-                    out=val_ps[b, chunk][:, t, :],
+                    out=val_ps[v][:, t, :],
                     lhsT=f_codes[b][:, keys].bitcast(FP8X4),
                     lhsT_scale=f_scales[b][:, keys],
                     rhs=w_codes[:, channels].bitcast(FP8X4),
@@ -152,24 +159,25 @@ def tile_mvpam_module_mask_cascade_pb_kernel(
                     stop=True,
                 )
 
-        def round_values(b, chunk):
-            g, ct = divmod(chunk, C_TILES)
+        def round_values(v):
+            b, g, ct = place_of_chunk(v)
             channels = slice(ct * P, (ct + 1) * P)
             nc.vector.tensor_tensor(
                 out=v_grp[b][:, g, channels, :],
-                in0=val_ps[b, chunk][:].rearrange("p t c -> p c t"),
+                in0=val_ps[v][:].rearrange("p t c -> p c t"),
                 in1=bias_all[:, channels].unsqueeze(2).to_broadcast([P, P, PACK]),
                 op=ALU.add,
             )
-            if ct == C_TILES - 1:
-                nc.vector.quantize_mx(
-                    out=v_codes[b][:, g, :].bitcast(FP8X4),
-                    scales=v_scales[b][:, g, :],
-                    in_=v_grp[b][:, g].rearrange("p c t -> p (c t)"),
-                )
 
-        s_ps, neg_max, e_sb, e_sums, e_grp, e_codes, e_scales = {}, {}, {}, {}, {}, {}, {}
-        eT_ps, inv_sum, acc, o_sb, oT_ps = {}, {}, {}, {}, {}
+        def quantise_values(b, g):
+            nc.vector.quantize_mx(
+                out=v_codes[b][:, g, :].bitcast(FP8X4),
+                scales=v_scales[b][:, g, :],
+                in_=v_grp[b][:, g].rearrange("p c t -> p (c t)"),
+            )
+
+        s_ps, bank_max, neg_max, e_sb, e_sums, e_grp, e_codes, e_scales = {}, {}, {}, {}, {}, {}, {}, {}
+        eT_ps, total, inv_sum, acc, o_sb, oT_ps = {}, {}, {}, {}, {}, {}
 
         def scores(i):
             b, mt = divmod(i, M_TILES)
@@ -183,13 +191,17 @@ def tile_mvpam_module_mask_cascade_pb_kernel(
                     stop=True,
                 )
 
-        def row_max(i):
-            bank_max = stats.tile([P, KEY_PASSES], F32, name="bank_max")
+        def bank_maxima(i):
+            bank_max[i] = stats.tile([P, KEY_PASSES], F32, name="bank_max")
             for g in range(KEY_PASSES):
-                nc.vector.reduce_max(out=bank_max[:, g : g + 1], in_=s_ps[i][:, g, :], axis=AXIS_X)
+                nc.vector.reduce_max(
+                    out=bank_max[i][:, g : g + 1], in_=s_ps[i][:, g, :], axis=AXIS_X
+                )
+
+        def join_maxima(i):
             neg_max[i] = stats.tile([P, 1], F32, name="neg_max")
             nc.vector.tensor_reduce(
-                out=neg_max[i][:], in_=bank_max[:], axis=AXIS_X, op=ALU.max, negate=True
+                out=neg_max[i][:], in_=bank_max[i][:], axis=AXIS_X, op=ALU.max, negate=True
             )
 
         def exponentials(i):
@@ -228,10 +240,14 @@ def tile_mvpam_module_mask_cascade_pb_kernel(
             nc.vector.quantize_mx(
                 out=e_codes[i][:].bitcast(FP8X4), scales=e_scales[i][:], in_=e_grp[i][:]
             )
-            total = stats.tile([P, 1], F32, name="total")
-            nc.vector.reduce_sum(out=total[:], in_=e_sums[i][:], axis=AXIS_X)
+
+        def add_sums(i):
+            total[i] = stats.tile([P, 1], F32, name="total")
+            nc.vector.reduce_sum(out=total[i][:], in_=e_sums[i][:], axis=AXIS_X)
+
+        def invert_sum(i):
             inv_sum[i] = stats.tile([P, 1], F32, name="inv_sum")
-            nc.vector.reciprocal(out=inv_sum[i][:], in_=total[:])
+            nc.vector.reciprocal(out=inv_sum[i][:], in_=total[i][:])
 
         def attend(i):
             b = i // M_TILES
@@ -275,33 +291,46 @@ def tile_mvpam_module_mask_cascade_pb_kernel(
                 out=out[b].rearrange("(t p) m -> p t m", p=P)[:, :, queries], in_=result[:]
             )
 
-        prepare_queries(0, nc.vector.tensor_copy)
-        scores(0)
+        prepare_queries(0, nc.scalar.copy)
         bias_ps = ps_work.tile([P, C], F32, name="bias_ps", tag="work")
         nc.tensor.matmul(out=bias_ps[:], lhsT=ones_bf[:], rhs=bias_row[:], start=True, stop=True)
         nc.scalar.copy(out=bias_all[:], in_=bias_ps[:])
-        nc.vector.tensor_copy(out=gamma_f32[:], in_=gamma_bf[:])
-        row_max(0)
         group_features(0, 0, nc.vector.tensor_copy)
         group_features(0, 1, nc.scalar.copy)
+        nc.gpsimd.tensor_copy(out=gamma_f32[:], in_=gamma_bf[:])
+
+        FIRST_STEP = -1
+        LAST_STEP = TILES - 1 + 3
 
         def live(i):
             return 0 <= i < TILES
 
-        def chunk_of_step(step):
-            before, chunk = divmod(step - 1, M_TILES)
-            return before + 1, chunk
-
-        for step in range(TILES + 3):
-            upcoming, chunk = chunk_of_step(step - 1)
-            if 1 <= upcoming < B:
-                round_values(upcoming, chunk)
+        multiplied = 0
+        rounded = 0
+        for step in range(FIRST_STEP, LAST_STEP + 1):
+            chunks_due = min(CHUNKS // 2 if step < FIRST_STEP + 2 else 1, B * CHUNKS - multiplied)
+            values_whole = None
+            if rounded < multiplied:
+                round_values(rounded)
+                b, g, ct = place_of_chunk(rounded)
+                if ct == C_TILES - 1:
+                    values_whole = (b, g)
+                rounded += 1
             if live(step - 3):
                 normalise(step - 3)
             if live(step + 1):
                 scores(step + 1)
             if live(step - 2):
+                add_sums(step - 2)
                 quantise_e(step - 2)
+            if values_whole is not None:
+                quantise_values(values_whole[0], values_whole[1])
+            if chunks_due > 0:
+                b, g, ct = place_of_chunk(multiplied)
+                if ct == 0:
+                    quantise_features(b, g)
+            if live(step - 2):
+                invert_sum(step - 2)
             if live(step):
                 exponentials(step)
             if live(step - 1):
@@ -309,21 +338,24 @@ def tile_mvpam_module_mask_cascade_pb_kernel(
             if live(step - 3):
                 flip_back(step - 3)
             if live(step + 1):
-                row_max(step + 1)
+                bank_maxima(step + 1)
             if live(step - 1):
                 gather_e(step - 1)
             if live(step - 2):
                 attend(step - 2)
             if live(step - 3):
                 finish(step - 3)
-            if step == 0:
-                for chunk in range(CHUNKS):
-                    multiply_values(0, chunk)
-                    round_values(0, chunk)
-            upcoming, chunk = chunk_of_step(step)
-            if 1 <= upcoming < B:
-                multiply_values(upcoming, chunk)
-            if step % M_TILES == 0 and step // M_TILES + 1 < B:
-                prepare_queries(step // M_TILES + 1, nc.scalar.copy)
+            if live(step + 1):
+                join_maxima(step + 1)
+            for unused in range(chunks_due):
+                multiply_values(multiplied)
+                multiplied += 1
+                if rounded < multiplied - 1:
+                    round_values(rounded)
+                    rounded += 1
+            upcoming = step // M_TILES + 1
+            if 0 < upcoming < B and step % M_TILES == 0:
                 for g in range(KEY_PASSES):
-                    group_features(step // M_TILES + 1, g, nc.scalar.copy)
+                    group_features(upcoming, g, nc.scalar.copy)
+            if 0 < upcoming < B and step % M_TILES == M_TILES // 2:
+                prepare_queries(upcoming, nc.scalar.copy)

@@ -111,13 +111,17 @@ def tile_mvpam_module_mask_cascade_pb_kernel(
         for b in range(B):
             nc.sync.dma_start(out=x_sb[b][:], in_=x[b].rearrange("(t p) m -> p t m", p=P))
 
-        def prepare_queries(b, copy):
-            flipped = ps_work.tile([P, M_TILES, P], BF16, name="qT_ps", tag="work")
+        qT_ps = {}
+
+        def flip_queries(b):
+            qT_ps[b] = ps_flip.tile([P, M_TILES, P], BF16, name="qT_ps", tag="flip")
             for i in range(M_TILES):
-                nc.tensor.transpose(flipped[:, i, :], q_sb[b][:, i, :], ident_bf[:])
-            copy(
+                nc.tensor.transpose(qT_ps[b][:, i, :], q_sb[b][:, i, :], ident_bf[:])
+
+        def copy_queries(b):
+            nc.scalar.copy(
                 out=qT[b][:].rearrange("d (p i) -> d p i", i=M_TILES),
-                in_=flipped[:].rearrange("d i p -> d p i"),
+                in_=qT_ps[b][:].rearrange("d i p -> d p i"),
             )
 
         def group_features(b, g, copy):
@@ -221,7 +225,7 @@ def tile_mvpam_module_mask_cascade_pb_kernel(
 
         def flip_e(i):
             words = e_sb[i][:].bitcast(F32)
-            eT_ps[i] = ps_flip.tile([P, 2 * KEY_PASSES, P], F32, name="eT_ps")
+            eT_ps[i] = ps_flip.tile([P, 2 * KEY_PASSES, P], F32, name="eT_ps", tag="flip")
             for gu in range(2 * KEY_PASSES):
                 nc.tensor.transpose(
                     eT_ps[i][:, gu, :], words[:, gu * P : (gu + 1) * P], ident_f32[:]
@@ -291,7 +295,8 @@ def tile_mvpam_module_mask_cascade_pb_kernel(
                 out=out[b].rearrange("(t p) m -> p t m", p=P)[:, :, queries], in_=result[:]
             )
 
-        prepare_queries(0, nc.scalar.copy)
+        flip_queries(0)
+        copy_queries(0)
         bias_ps = ps_work.tile([P, C], F32, name="bias_ps", tag="work")
         nc.tensor.matmul(out=bias_ps[:], lhsT=ones_bf[:], rhs=bias_row[:], start=True, stop=True)
         nc.scalar.copy(out=bias_all[:], in_=bias_ps[:])
@@ -300,7 +305,7 @@ def tile_mvpam_module_mask_cascade_pb_kernel(
         nc.gpsimd.tensor_copy(out=gamma_f32[:], in_=gamma_bf[:])
 
         FIRST_STEP = -1
-        LAST_STEP = TILES - 1 + 3
+        LAST_STEP = TILES - 1 + 4
 
         def live(i):
             return 0 <= i < TILES
@@ -309,7 +314,12 @@ def tile_mvpam_module_mask_cascade_pb_kernel(
         rounded = 0
         for step in range(FIRST_STEP, LAST_STEP + 1):
             chunks_due = min(CHUNKS // 2 if step < FIRST_STEP + 2 else 1, B * CHUNKS - multiplied)
+            upcoming = step // M_TILES + 1
+            place_in_batch = step % M_TILES
             values_whole = None
+            if live(step - 2):
+                add_sums(step - 2)
+                quantise_e(step - 2)
             if rounded < multiplied:
                 round_values(rounded)
                 b, g, ct = place_of_chunk(rounded)
@@ -318,44 +328,41 @@ def tile_mvpam_module_mask_cascade_pb_kernel(
                 rounded += 1
             if live(step - 3):
                 normalise(step - 3)
+            if 0 < upcoming < B and place_in_batch == M_TILES // 2 + 1:
+                copy_queries(upcoming)
             if live(step + 1):
                 scores(step + 1)
             if live(step - 2):
-                add_sums(step - 2)
-                quantise_e(step - 2)
+                invert_sum(step - 2)
             if values_whole is not None:
                 quantise_values(values_whole[0], values_whole[1])
             if chunks_due > 0:
                 b, g, ct = place_of_chunk(multiplied)
                 if ct == 0:
                     quantise_features(b, g)
-            if live(step - 2):
-                invert_sum(step - 2)
             if live(step):
                 exponentials(step)
             if live(step - 1):
                 flip_e(step - 1)
-            if live(step - 3):
-                flip_back(step - 3)
-            if live(step + 1):
-                bank_maxima(step + 1)
-            if live(step - 1):
-                gather_e(step - 1)
+            if live(step - 4):
+                finish(step - 4)
             if live(step - 2):
                 attend(step - 2)
-            if live(step - 3):
-                finish(step - 3)
             if live(step + 1):
+                bank_maxima(step + 1)
                 join_maxima(step + 1)
+            if live(step - 1):
+                gather_e(step - 1)
+            if live(step - 3):
+                flip_back(step - 3)
             for unused in range(chunks_due):
                 multiply_values(multiplied)
                 multiplied += 1
                 if rounded < multiplied - 1:
                     round_values(rounded)
                     rounded += 1
-            upcoming = step // M_TILES + 1
-            if 0 < upcoming < B and step % M_TILES == 0:
+            if 0 < upcoming < B and place_in_batch == M_TILES // 2:
+                flip_queries(upcoming)
+            if 0 < upcoming < B and place_in_batch == 0:
                 for g in range(KEY_PASSES):
                     group_features(upcoming, g, nc.scalar.copy)
-            if 0 < upcoming < B and step % M_TILES == M_TILES // 2:
-                prepare_queries(upcoming, nc.scalar.copy)

@@ -50,7 +50,8 @@ def tile_mvpam_module_mask_cascade_pb_kernel(
             q_sb[b] = batch.tile([P, M_TILES, D], BF16, name="q_sb%d" % b)
             qT[b] = batch.tile([P, N], BF16, name="qT%d" % b)
             x_sb[b] = batch.tile([P, C_TILES, N], BF16, name="x_sb%d" % b)
-            f_raw[b] = batch.tile([P, PACK, N], BF16, name="f_raw%d" % b)
+            for g in range(KEY_PASSES):
+                f_raw[b, g] = batch.tile([P, PACK, K_PASS], BF16, name="f_raw%d_%d" % (b, g))
             f_grp[b] = batch.tile(
                 [P, KEY_PASSES, PACK, P, PACK], BF16, name="f_grp%d" % b, align_bytes=64
             )
@@ -87,7 +88,7 @@ def tile_mvpam_module_mask_cascade_pb_kernel(
         def load_features(b, g):
             keys = slice(g * K_PASS, (g + 1) * K_PASS)
             nc.sync.dma_start(
-                out=f_raw[b][:, :, keys],
+                out=f_raw[b, g][:],
                 in_=out1[b].rearrange("(p j) n -> p j n", j=PACK)[:, :, keys],
             )
 
@@ -127,9 +128,7 @@ def tile_mvpam_module_mask_cascade_pb_kernel(
         def group_features(b, g, copy):
             copy(
                 out=f_grp[b][:, g],
-                in_=f_raw[b][:, :, g * K_PASS : (g + 1) * K_PASS].rearrange(
-                    "p j (r t) -> p t r j", t=PACK
-                ),
+                in_=f_raw[b, g][:].rearrange("p j (r t) -> p t r j", t=PACK),
             )
 
         def quantise_features(b, g):
@@ -247,7 +246,9 @@ def tile_mvpam_module_mask_cascade_pb_kernel(
 
         def add_sums(i):
             total[i] = stats.tile([P, 1], F32, name="total")
-            nc.vector.reduce_sum(out=total[i][:], in_=e_sums[i][:], axis=AXIS_X)
+            nc.gpsimd.tensor_tensor(
+                out=total[i][:], in0=e_sums[i][:, 0:1], in1=e_sums[i][:, 1:2], op=ALU.add
+            )
 
         def invert_sum(i):
             inv_sum[i] = stats.tile([P, 1], F32, name="inv_sum")
@@ -318,8 +319,9 @@ def tile_mvpam_module_mask_cascade_pb_kernel(
             place_in_batch = step % M_TILES
             values_whole = None
             if live(step - 2):
-                add_sums(step - 2)
                 quantise_e(step - 2)
+            if live(step - 4):
+                finish(step - 4)
             if rounded < multiplied:
                 round_values(rounded)
                 b, g, ct = place_of_chunk(rounded)
@@ -342,10 +344,9 @@ def tile_mvpam_module_mask_cascade_pb_kernel(
                     quantise_features(b, g)
             if live(step):
                 exponentials(step)
+                add_sums(step)
             if live(step - 1):
                 flip_e(step - 1)
-            if live(step - 4):
-                finish(step - 4)
             if live(step - 2):
                 attend(step - 2)
             if live(step + 1):

@@ -127,8 +127,8 @@ def tile_mvpam_module_mask_cascade_pb_kernel(
 
         def group_features(b, g, copy):
             copy(
-                out=f_grp[b][:, g],
-                in_=f_raw[b, g][:].rearrange("p j (r t) -> p t r j", t=PACK),
+                out=f_grp[b][:, g].rearrange("p t (c i) j -> p (t c) j i", i=4),
+                in_=f_raw[b, g][:].rearrange("p j (c i) -> p c j i", i=4),
             )
 
         def quantise_features(b, g):
@@ -215,7 +215,7 @@ def tile_mvpam_module_mask_cascade_pb_kernel(
                     out=e_sb[i][:, g * K_PASS : (g + 1) * K_PASS].rearrange(
                         "m (u r e) -> m u r e", u=2, e=2
                     ),
-                    in_=s_ps[i][:, g, :].rearrange("m (r u e) -> m u r e", u=2, e=2),
+                    in_=s_ps[i][:, g, :].rearrange("m (u e r) -> m u r e", u=2, e=2),
                     func=ACT.Exp,
                     bias=neg_max[i][:, 0:1],
                     scale=1.0,

@@ -184,10 +184,10 @@ def tile_mvpam_module_mask_cascade_pb_kernel(
 
         def scores(i):
             b, mt = divmod(i, M_TILES)
-            s_ps[i] = ps_scores.tile([P, KEY_PASSES, BANK], F32, name="s_ps")
             for g in range(KEY_PASSES):
+                s_ps[i, g] = ps_scores.tile([P, BANK], F32, name="s_ps", tag="s_ps%d" % g)
                 nc.tensor.matmul(
-                    out=s_ps[i][:, g, :],
+                    out=s_ps[i, g][:],
                     lhsT=qT[b][:, mt * P : (mt + 1) * P],
                     rhs=k_sb[b][:, g * BANK : (g + 1) * BANK],
                     start=True,
@@ -198,7 +198,7 @@ def tile_mvpam_module_mask_cascade_pb_kernel(
             bank_max[i] = stats.tile([P, KEY_PASSES], F32, name="bank_max")
             for g in range(KEY_PASSES):
                 nc.vector.reduce_max(
-                    out=bank_max[i][:, g : g + 1], in_=s_ps[i][:, g, :], axis=AXIS_X
+                    out=bank_max[i][:, g : g + 1], in_=s_ps[i, g][:], axis=AXIS_X
                 )
 
         def join_maxima(i):
@@ -215,34 +215,52 @@ def tile_mvpam_module_mask_cascade_pb_kernel(
                     out=e_sb[i][:, g * K_PASS : (g + 1) * K_PASS].rearrange(
                         "m (u r e) -> m u r e", u=2, e=2
                     ),
-                    in_=s_ps[i][:, g, :].rearrange("m (u e r) -> m u r e", u=2, e=2),
+                    in_=s_ps[i, g][:].rearrange("m (u e r) -> m u r e", u=2, e=2),
                     func=ACT.Exp,
                     bias=neg_max[i][:, 0:1],
                     scale=1.0,
                     accum_out=e_sums[i][:, g : g + 1],
                 )
 
+        def parts(i):
+            return 2 if i == TILES - 1 else 1
+
         def flip_e(i):
             words = e_sb[i][:].bitcast(F32)
-            eT_ps[i] = ps_flip.tile([P, 2 * KEY_PASSES, P], F32, name="eT_ps", tag="flip")
-            for gu in range(2 * KEY_PASSES):
-                nc.tensor.transpose(
-                    eT_ps[i][:, gu, :], words[:, gu * P : (gu + 1) * P], ident_f32[:]
-                )
+            count = 2 * KEY_PASSES // parts(i)
+            for h in range(parts(i)):
+                if h == 0:
+                    eT_ps[i, h] = ps_flip.tile([P, count, P], F32, name="eT_ps", tag="flip")
+                else:
+                    eT_ps[i, h] = ps_scores.tile([P, count, P], F32, name="eT_ps", tag="s_ps0")
+                for w in range(count):
+                    first = (h * count + w) * P
+                    nc.tensor.transpose(
+                        eT_ps[i, h][:, w, :], words[:, first : first + P], ident_f32[:]
+                    )
 
         def gather_e(i):
             e_grp[i] = stream.tile([P, N], BF16, name="e_grp", align_bytes=64)
-            nc.scalar.copy(
-                out=e_grp[i][:].bitcast(F32).rearrange("r (g m u) -> r g m u", g=KEY_PASSES, u=2),
-                in_=eT_ps[i][:].rearrange("r (g u) m -> r g m u", g=KEY_PASSES),
-            )
+            keys = N // parts(i)
+            for h in range(parts(i)):
+                nc.scalar.copy(
+                    out=e_grp[i][:, h * keys : (h + 1) * keys]
+                    .bitcast(F32)
+                    .rearrange("r (g m u) -> r g m u", u=2, m=P),
+                    in_=eT_ps[i, h][:].rearrange("r (g u) m -> r g m u", u=2),
+                )
 
         def quantise_e(i):
             e_codes[i] = stream.tile([P, KEY_PASSES * P], U32, name="e_codes", align_bytes=64)
             e_scales[i] = stream.tile([P, KEY_PASSES * P], U8, name="e_scales", align_bytes=64)
-            nc.vector.quantize_mx(
-                out=e_codes[i][:].bitcast(FP8X4), scales=e_scales[i][:], in_=e_grp[i][:]
-            )
+            words = KEY_PASSES * P // parts(i)
+            for h in range(parts(i)):
+                piece = slice(h * words, (h + 1) * words)
+                nc.vector.quantize_mx(
+                    out=e_codes[i][:, piece].bitcast(FP8X4),
+                    scales=e_scales[i][:, piece],
+                    in_=e_grp[i][:, h * words * PACK : (h + 1) * words * PACK],
+                )
 
         def add_sums(i):
             total[i] = stats.tile([P, 1], F32, name="total")
@@ -256,45 +274,63 @@ def tile_mvpam_module_mask_cascade_pb_kernel(
 
         def attend(i):
             b = i // M_TILES
-            acc[i] = ps_work.tile([P, C], F32, name="acc", tag="work")
-            for g in range(KEY_PASSES):
-                queries = slice(g * P, (g + 1) * P)
-                nc.tensor.matmul_mx(
-                    out=acc[i][:],
-                    lhsT=e_codes[i][:, queries].bitcast(FP8X4),
-                    lhsT_scale=e_scales[i][:, queries],
-                    rhs=v_codes[b][:, g, :].bitcast(FP8X4),
-                    rhs_scale=v_scales[b][:, g, :],
-                    start=(g == 0),
-                    stop=(g == KEY_PASSES - 1),
-                )
+            width = C // parts(i)
+            for h in range(parts(i)):
+                channels = slice(h * width, (h + 1) * width)
+                if h == 0:
+                    acc[i, h] = ps_work.tile([P, width], F32, name="acc", tag="work")
+                else:
+                    acc[i, h] = ps_scores.tile([P, width], F32, name="acc", tag="s_ps1")
+                for g in range(KEY_PASSES):
+                    queries = slice(g * P, (g + 1) * P)
+                    nc.tensor.matmul_mx(
+                        out=acc[i, h][:],
+                        lhsT=e_codes[i][:, queries].bitcast(FP8X4),
+                        lhsT_scale=e_scales[i][:, queries],
+                        rhs=v_codes[b][:, g, channels].bitcast(FP8X4),
+                        rhs_scale=v_scales[b][:, g, channels],
+                        start=(g == 0),
+                        stop=(g == KEY_PASSES - 1),
+                    )
 
         def normalise(i):
-            o_sb[i] = stream.tile([P, C], F32, name="o_sb")
-            nc.scalar.activation(out=o_sb[i][:], in_=acc[i][:], func=ACT.Copy, scale=inv_sum[i][:, 0:1])
+            width = C // parts(i)
+            for h in range(parts(i)):
+                o_sb[i, h] = stream.tile([P, width], F32, name="o_sb", tag="o_sb%d" % h)
+                nc.scalar.activation(
+                    out=o_sb[i, h][:], in_=acc[i, h][:], func=ACT.Copy, scale=inv_sum[i][:, 0:1]
+                )
 
         def flip_back(i):
-            oT_ps[i] = ps_work.tile([P, C_TILES, P], F32, name="oT_ps", tag="work")
-            for ct in range(C_TILES):
-                nc.tensor.transpose(
-                    oT_ps[i][:, ct, :], o_sb[i][:, ct * P : (ct + 1) * P], ident_f32[:]
-                )
+            count = C_TILES // parts(i)
+            for h in range(parts(i)):
+                if h == 0:
+                    oT_ps[i, h] = ps_work.tile([P, count, P], F32, name="oT_ps", tag="work")
+                else:
+                    oT_ps[i, h] = ps_scores.tile([P, count, P], F32, name="oT_ps", tag="s_ps0")
+                for ct in range(count):
+                    nc.tensor.transpose(
+                        oT_ps[i, h][:, ct, :], o_sb[i, h][:, ct * P : (ct + 1) * P], ident_f32[:]
+                    )
 
         def finish(i):
             b, mt = divmod(i, M_TILES)
             queries = slice(mt * P, (mt + 1) * P)
-            result = stream.tile([P, C_TILES, P], F32, name="result", bufs=3)
-            nc.vector.scalar_tensor_tensor(
-                out=result[:],
-                in0=oT_ps[i][:],
-                scalar=gamma_f32[:, 0:1],
-                in1=x_sb[b][:, :, queries],
-                op0=ALU.mult,
-                op1=ALU.add,
-            )
-            nc.sync.dma_start(
-                out=out[b].rearrange("(t p) m -> p t m", p=P)[:, :, queries], in_=result[:]
-            )
+            count = C_TILES // parts(i)
+            for h in range(parts(i)):
+                cts = slice(h * count, (h + 1) * count)
+                result = stream.tile([P, count, P], F32, name="result", bufs=5)
+                nc.vector.scalar_tensor_tensor(
+                    out=result[:],
+                    in0=oT_ps[i, h][:],
+                    scalar=gamma_f32[:, 0:1],
+                    in1=x_sb[b][:, cts, queries],
+                    op0=ALU.mult,
+                    op1=ALU.add,
+                )
+                nc.sync.dma_start(
+                    out=out[b].rearrange("(t p) m -> p t m", p=P)[:, cts, queries], in_=result[:]
+                )
 
         flip_queries(0)
         copy_queries(0)
@@ -334,8 +370,8 @@ def tile_mvpam_module_mask_cascade_pb_kernel(
                 copy_queries(upcoming)
             if live(step + 1):
                 scores(step + 1)
-            if live(step - 2):
-                invert_sum(step - 2)
+            if live(step - 1):
+                invert_sum(step - 1)
             if values_whole is not None:
                 quantise_values(values_whole[0], values_whole[1])
             if chunks_due > 0:

@@ -347,59 +347,51 @@ def tile_mvpam_module_mask_cascade_pb_kernel(
         def live(i):
             return 0 <= i < TILES
 
-        multiplied = 0
-        rounded = 0
+        made = 0
+        whole = None
         for step in range(FIRST_STEP, LAST_STEP + 1):
-            chunks_due = min(CHUNKS // 2 if step < FIRST_STEP + 2 else 1, B * CHUNKS - multiplied)
-            upcoming = step // M_TILES + 1
-            place_in_batch = step % M_TILES
-            values_whole = None
             if live(step - 2):
                 quantise_e(step - 2)
-            if live(step - 4):
-                finish(step - 4)
-            if rounded < multiplied:
-                round_values(rounded)
-                b, g, ct = place_of_chunk(rounded)
-                if ct == C_TILES - 1:
-                    values_whole = (b, g)
-                rounded += 1
-            if live(step - 3):
-                normalise(step - 3)
-            if 0 < upcoming < B and place_in_batch == M_TILES // 2 + 1:
-                copy_queries(upcoming)
+            due = min(C_TILES if step < FIRST_STEP + 2 else 1, B * CHUNKS - made)
+            if due > 0 and made % C_TILES == 0:
+                b, g, ct = place_of_chunk(made)
+                quantise_features(b, g)
             if live(step + 1):
                 scores(step + 1)
+                bank_maxima(step + 1)
+            for v in range(made, made + due):
+                multiply_values(v)
+                if v > made:
+                    round_values(v - 1)
+            made += due
+            if live(step - 4):
+                flip_back(step - 4)
+            if step in (0, 1):
+                group_features(1, step, nc.scalar.copy)
+            if live(step - 3):
+                normalise(step - 3)
+            if step == M_TILES - 3:
+                copy_queries(1)
+            if whole is not None:
+                quantise_values(whole[0], whole[1])
+                whole = None
+            if due > 0:
+                round_values(made - 1)
+                if made % C_TILES == 0:
+                    whole = place_of_chunk(made - 1)
             if live(step - 1):
+                flip_e(step - 1)
                 invert_sum(step - 1)
-            if values_whole is not None:
-                quantise_values(values_whole[0], values_whole[1])
-            if chunks_due > 0:
-                b, g, ct = place_of_chunk(multiplied)
-                if ct == 0:
-                    quantise_features(b, g)
+            if live(step - 2):
+                attend(step - 2)
             if live(step):
                 exponentials(step)
                 add_sums(step)
-            if live(step - 1):
-                flip_e(step - 1)
-            if live(step - 2):
-                attend(step - 2)
             if live(step + 1):
-                bank_maxima(step + 1)
                 join_maxima(step + 1)
+            if live(step - 4):
+                finish(step - 4)
+            if step == M_TILES - 4:
+                flip_queries(1)
             if live(step - 1):
                 gather_e(step - 1)
-            if live(step - 3):
-                flip_back(step - 3)
-            for unused in range(chunks_due):
-                multiply_values(multiplied)
-                multiplied += 1
-                if rounded < multiplied - 1:
-                    round_values(rounded)
-                    rounded += 1
-            if 0 < upcoming < B and place_in_batch == M_TILES // 2:
-                flip_queries(upcoming)
-            if 0 < upcoming < B and place_in_batch == 0:
-                for g in range(KEY_PASSES):
-                    group_features(upcoming, g, nc.scalar.copy)

@@ -36,7 +36,7 @@ def tile_mvpam_module_mask_cascade_pb_kernel(
         const = ctx.enter_context(tc.tile_pool(name="const", bufs=1))
         batch = ctx.enter_context(tc.tile_pool(name="batch", bufs=1))
         stream = ctx.enter_context(tc.tile_pool(name="stream", bufs=2))
-        stats = ctx.enter_context(tc.tile_pool(name="stats", bufs=3))
+        stats = ctx.enter_context(tc.tile_pool(name="stats", bufs=8))
         ps_scores = ctx.enter_context(tc.psum_pool(name="ps_scores", bufs=2))
         ps_flip = ctx.enter_context(tc.psum_pool(name="ps_flip", bufs=1))
         ps_work = ctx.enter_context(tc.psum_pool(name="ps_work", bufs=3))
@@ -79,11 +79,13 @@ def tile_mvpam_module_mask_cascade_pb_kernel(
         make_identity(nc, ident_bf[:])
         make_identity(nc, ident_f32[:])
 
-        def load_scores_operands(b):
-            nc.sync.dma_start(out=k_sb[b][:], in_=k[b])
+        def load_queries(b):
             nc.sync.dma_start(
                 out=q_sb[b][:], in_=q[b].rearrange("(p i) d -> p i d", i=M_TILES)
             )
+
+        def load_keys(b):
+            nc.sync.dma_start(out=k_sb[b][:], in_=k[b])
 
         def load_features(b, g):
             keys = slice(g * K_PASS, (g + 1) * K_PASS)
@@ -92,8 +94,9 @@ def tile_mvpam_module_mask_cascade_pb_kernel(
                 in_=out1[b].rearrange("(p j) n -> p j n", j=PACK)[:, :, keys],
             )
 
-        load_scores_operands(0)
+        load_queries(0)
         load_features(0, 0)
+        load_keys(0)
         nc.sync.dma_start(
             out=w_codes[:].bitcast(I32),
             in_=wv2_words[0].rearrange("p n t -> p (n t)").bitcast(I32),
@@ -105,7 +108,8 @@ def tile_mvpam_module_mask_cascade_pb_kernel(
             )
         nc.sync.dma_start(out=bias_row[0:1, :], in_=bv2.unsqueeze(0))
         load_features(0, 1)
-        load_scores_operands(1)
+        load_queries(1)
+        load_keys(1)
         load_features(1, 0)
         load_features(1, 1)
         nc.sync.dma_start(out=gamma_bf[:], in_=gamma.partition_broadcast(P))
@@ -120,10 +124,12 @@ def tile_mvpam_module_mask_cascade_pb_kernel(
                 nc.tensor.transpose(qT_ps[b][:, i, :], q_sb[b][:, i, :], ident_bf[:])
 
         def copy_queries(b):
-            nc.scalar.copy(
-                out=qT[b][:].rearrange("d (p i) -> d p i", i=M_TILES),
-                in_=qT_ps[b][:].rearrange("d i p -> d p i"),
-            )
+            edges = (0, P // M_TILES, P) if b == 0 else (0, P)
+            for lo, hi in zip(edges[:-1], edges[1:]):
+                nc.scalar.copy(
+                    out=qT[b][:].rearrange("d (p i) -> d p i", i=M_TILES)[:, lo:hi],
+                    in_=qT_ps[b][:].rearrange("d i p -> d p i")[:, lo:hi],
+                )
 
         def group_features(b, g, copy):
             copy(
@@ -138,6 +144,11 @@ def tile_mvpam_module_mask_cascade_pb_kernel(
                 scales=f_scales[b][:, cols],
                 in_=f_grp[b][:, g].rearrange("p t r j -> p (t r j)"),
             )
+
+        def spread_bias():
+            bias_ps = ps_work.tile([P, C], F32, name="bias_ps", tag="work")
+            nc.tensor.matmul(out=bias_ps[:], lhsT=ones_bf[:], rhs=bias_row[:], start=True, stop=True)
+            nc.scalar.copy(out=bias_all[:], in_=bias_ps[:])
 
         val_ps = {}
 
@@ -319,7 +330,7 @@ def tile_mvpam_module_mask_cascade_pb_kernel(
             count = C_TILES // parts(i)
             for h in range(parts(i)):
                 cts = slice(h * count, (h + 1) * count)
-                result = stream.tile([P, count, P], F32, name="result", bufs=5)
+                result = stream.tile([P, count, P], F32, name="result", bufs=TILES + 1)
                 nc.vector.scalar_tensor_tensor(
                     out=result[:],
                     in0=oT_ps[i, h][:],
@@ -334,11 +345,7 @@ def tile_mvpam_module_mask_cascade_pb_kernel(
 
         flip_queries(0)
         copy_queries(0)
-        bias_ps = ps_work.tile([P, C], F32, name="bias_ps", tag="work")
-        nc.tensor.matmul(out=bias_ps[:], lhsT=ones_bf[:], rhs=bias_row[:], start=True, stop=True)
-        nc.scalar.copy(out=bias_all[:], in_=bias_ps[:])
         group_features(0, 0, nc.vector.tensor_copy)
-        group_features(0, 1, nc.scalar.copy)
         nc.gpsimd.tensor_copy(out=gamma_f32[:], in_=gamma_bf[:])
 
         FIRST_STEP = -1
@@ -359,6 +366,9 @@ def tile_mvpam_module_mask_cascade_pb_kernel(
             if live(step + 1):
                 scores(step + 1)
                 bank_maxima(step + 1)
+            if step == FIRST_STEP:
+                spread_bias()
+                group_features(0, 1, nc.scalar.copy)
             for v in range(made, made + due):
                 multiply_values(v)
                 if v > made:

@@ -25,6 +25,8 @@ M_TILES = N // P
 TILES = B * M_TILES
 CHUNKS = KEY_PASSES * C_TILES
 
+WARM_UPS = 5
+
 FLOPS = B * (2 * C * C * N + 2 * N * N * D + 2 * C * N * N)
 
 
@@ -35,8 +37,8 @@ def tile_mvpam_module_mask_cascade_pb_kernel(
     with ExitStack() as ctx:
         const = ctx.enter_context(tc.tile_pool(name="const", bufs=1))
         batch = ctx.enter_context(tc.tile_pool(name="batch", bufs=1))
-        stream = ctx.enter_context(tc.tile_pool(name="stream", bufs=2))
-        stats = ctx.enter_context(tc.tile_pool(name="stats", bufs=8))
+        stream = ctx.enter_context(tc.tile_pool(name="stream", bufs=4))
+        stats = ctx.enter_context(tc.tile_pool(name="stats", bufs=TILES))
         ps_scores = ctx.enter_context(tc.psum_pool(name="ps_scores", bufs=2))
         ps_flip = ctx.enter_context(tc.psum_pool(name="ps_flip", bufs=1))
         ps_work = ctx.enter_context(tc.psum_pool(name="ps_work", bufs=3))
@@ -69,13 +71,15 @@ def tile_mvpam_module_mask_cascade_pb_kernel(
         ident_f32 = const.tile([P, P], F32, name="ident_f32")
         ones_bf = const.tile([P, P], BF16, name="ones_bf")
         bias_row = const.tile([P, C], BF16, name="bias_row")
+        zero_row = const.tile([P, BANK], BF16, name="zero_row")
         bias_all = const.tile([P, C], F32, name="bias_all")
         gamma_bf = const.tile([P, 1], BF16, name="gamma_bf")
         gamma_f32 = const.tile([P, 1], F32, name="gamma_f32")
 
+        nc.vector.memset(ones_bf[:], 1.0)
+        nc.vector.memset(zero_row[:], 0.0)
         nc.vector.memset(w_scales[:].bitcast(I32), 0)
         nc.vector.memset(bias_row[:], 0.0)
-        nc.vector.memset(ones_bf[:], 1.0)
         make_identity(nc, ident_bf[:])
         make_identity(nc, ident_f32[:])
 
@@ -240,21 +244,21 @@ def tile_mvpam_module_mask_cascade_pb_kernel(
             words = e_sb[i][:].bitcast(F32)
             count = 2 * KEY_PASSES // parts(i)
             for h in range(parts(i)):
-                if h == 0:
+                if parts(i) == 1:
                     eT_ps[i, h] = ps_flip.tile([P, count, P], F32, name="eT_ps", tag="flip")
                 else:
-                    eT_ps[i, h] = ps_scores.tile([P, count, P], F32, name="eT_ps", tag="s_ps0")
+                    eT_ps[i, h] = ps_scores.tile([P, count, P], F32, name="eT_ps", tag="s_ps%d" % h)
                 for w in range(count):
                     first = (h * count + w) * P
                     nc.tensor.transpose(
                         eT_ps[i, h][:, w, :], words[:, first : first + P], ident_f32[:]
                     )
 
-        def gather_e(i):
+        def gather_e(i, copy=nc.scalar.copy):
             e_grp[i] = stream.tile([P, N], BF16, name="e_grp", align_bytes=64)
             keys = N // parts(i)
             for h in range(parts(i)):
-                nc.scalar.copy(
+                copy(
                     out=e_grp[i][:, h * keys : (h + 1) * keys]
                     .bitcast(F32)
                     .rearrange("r (g m u) -> r g m u", u=2, m=P),
@@ -304,13 +308,17 @@ def tile_mvpam_module_mask_cascade_pb_kernel(
                         stop=(g == KEY_PASSES - 1),
                     )
 
-        def normalise(i):
+        def times_on_scalar(out, in_, factor):
+            nc.scalar.activation(out=out, in_=in_, func=ACT.Copy, scale=factor)
+
+        def times_on_vector(out, in_, factor):
+            nc.vector.tensor_scalar(out=out, in0=in_, scalar1=factor, scalar2=None, op0=ALU.mult)
+
+        def normalise(i, times=times_on_scalar):
             width = C // parts(i)
             for h in range(parts(i)):
                 o_sb[i, h] = stream.tile([P, width], F32, name="o_sb", tag="o_sb%d" % h)
-                nc.scalar.activation(
-                    out=o_sb[i, h][:], in_=acc[i, h][:], func=ACT.Copy, scale=inv_sum[i][:, 0:1]
-                )
+                times(o_sb[i, h][:], acc[i, h][:], inv_sum[i][:, 0:1])
 
         def flip_back(i):
             count = C_TILES // parts(i)
@@ -343,20 +351,23 @@ def tile_mvpam_module_mask_cascade_pb_kernel(
                     out=out[b].rearrange("(t p) m -> p t m", p=P)[:, cts, queries], in_=result[:]
                 )
 
+        warm_ps = ps_work.tile([P, BANK], F32, name="warm_ps", tag="work")
+        for unused in range(WARM_UPS):
+            nc.tensor.matmul(out=warm_ps[:], lhsT=ones_bf[:], rhs=zero_row[:], start=True, stop=True)
         flip_queries(0)
         copy_queries(0)
         group_features(0, 0, nc.vector.tensor_copy)
         nc.gpsimd.tensor_copy(out=gamma_f32[:], in_=gamma_bf[:])
 
         FIRST_STEP = -1
-        LAST_STEP = TILES - 1 + 4
+        LAST = TILES - 1
 
         def live(i):
             return 0 <= i < TILES
 
         made = 0
         whole = None
-        for step in range(FIRST_STEP, LAST_STEP + 1):
+        for step in range(FIRST_STEP, LAST):
             if live(step - 2):
                 quantise_e(step - 2)
             due = min(C_TILES if step < FIRST_STEP + 2 else 1, B * CHUNKS - made)
@@ -405,3 +416,32 @@ def tile_mvpam_module_mask_cascade_pb_kernel(
                 flip_queries(1)
             if live(step - 1):
                 gather_e(step - 1)
+
+        quantise_e(LAST - 2)
+        flip_e(LAST - 1)
+        flip_back(LAST - 4)
+        normalise(LAST - 3)
+        exponentials(LAST)
+        add_sums(LAST)
+        attend(LAST - 2)
+        flip_back(LAST - 3)
+        invert_sum(LAST - 1)
+        gather_e(LAST - 1, nc.vector.tensor_copy)
+        flip_e(LAST)
+        normalise(LAST - 2)
+        finish(LAST - 4)
+        gather_e(LAST)
+        quantise_e(LAST - 1)
+        attend(LAST - 1)
+        invert_sum(LAST)
+        finish(LAST - 3)
+        flip_back(LAST - 2)
+        quantise_e(LAST)
+        normalise(LAST - 1, times_on_vector)
+        attend(LAST)
+        normalise(LAST)
+        finish(LAST - 2)
+        flip_back(LAST - 1)
+        flip_back(LAST)
+        finish(LAST - 1)
+        finish(LAST)

from contextlib import ExitStack

import concourse.mybir as mybir
from concourse.masks import make_identity

F32 = mybir.dt.float32
BF16 = mybir.dt.bfloat16
I32 = mybir.dt.int32
U32 = mybir.dt.uint32
U8 = mybir.dt.uint8
FP8X4 = mybir.dt.float8_e4m3fn_x4
ALU = mybir.AluOpType
ACT = mybir.ActivationFunctionType
AXIS_X = mybir.AxisListType.X

P = 128
PACK = 4
K_PASS = P * PACK
BANK = 512

B, C, D, N = 2, 512, 128, 1024
KEY_PASSES = N // K_PASS
C_TILES = C // P
M_TILES = N // P
TILES = B * M_TILES
CHUNKS = KEY_PASSES * C_TILES

WARM_UPS = 5

FLOPS = B * (2 * C * C * N + 2 * N * N * D + 2 * C * N * N)


def tile_mvpam_module_mask_cascade_pb_kernel(
    tc, x, out1, q, k, wv2_words, wv2_scales, bv2, gamma, out
):
    nc = tc.nc
    with ExitStack() as ctx:
        const = ctx.enter_context(tc.tile_pool(name="const", bufs=1))
        batch = ctx.enter_context(tc.tile_pool(name="batch", bufs=1))
        stream = ctx.enter_context(tc.tile_pool(name="stream", bufs=4))
        stats = ctx.enter_context(tc.tile_pool(name="stats", bufs=TILES))
        ps_scores = ctx.enter_context(tc.psum_pool(name="ps_scores", bufs=2))
        ps_flip = ctx.enter_context(tc.psum_pool(name="ps_flip", bufs=1))
        ps_work = ctx.enter_context(tc.psum_pool(name="ps_work", bufs=3))
        ctx.enter_context(tc.manual_schedule())

        k_sb, q_sb, qT, x_sb = {}, {}, {}, {}
        f_raw, f_grp, f_codes, f_scales = {}, {}, {}, {}
        v_grp, v_codes, v_scales = {}, {}, {}
        for b in range(B):
            k_sb[b] = batch.tile([P, N], BF16, name="k_sb%d" % b)
            q_sb[b] = batch.tile([P, M_TILES, D], BF16, name="q_sb%d" % b)
            qT[b] = batch.tile([P, N], BF16, name="qT%d" % b)
            x_sb[b] = batch.tile([P, C_TILES, N], BF16, name="x_sb%d" % b)
            for g in range(KEY_PASSES):
                f_raw[b, g] = batch.tile([P, PACK, K_PASS], BF16, name="f_raw%d_%d" % (b, g))
            f_grp[b] = batch.tile(
                [P, KEY_PASSES, PACK, P, PACK], BF16, name="f_grp%d" % b, align_bytes=64
            )
            f_codes[b] = batch.tile([P, N], U32, name="f_codes%d" % b, align_bytes=64)
            f_scales[b] = batch.tile([P, N], U8, name="f_scales%d" % b, align_bytes=64)
            v_grp[b] = batch.tile(
                [P, KEY_PASSES, C, PACK], BF16, name="v_grp%d" % b, align_bytes=64
            )
            v_codes[b] = batch.tile([P, KEY_PASSES, C], U32, name="v_codes%d" % b, align_bytes=64)
            v_scales[b] = batch.tile([P, KEY_PASSES, C], U8, name="v_scales%d" % b, align_bytes=64)

        w_codes = const.tile([P, C], U32, name="w_codes", align_bytes=64)
        w_scales = const.tile([P, C], U8, name="w_scales", align_bytes=64)
        ident_bf = const.tile([P, P], BF16, name="ident_bf")
        ident_f32 = const.tile([P, P], F32, name="ident_f32")
        ones_bf = const.tile([P, P], BF16, name="ones_bf")
        bias_row = const.tile([P, C], BF16, name="bias_row")
        zero_row = const.tile([P, BANK], BF16, name="zero_row")
        bias_all = const.tile([P, C], F32, name="bias_all")
        gamma_bf = const.tile([P, 1], BF16, name="gamma_bf")
        gamma_f32 = const.tile([P, 1], F32, name="gamma_f32")

        nc.vector.memset(ones_bf[:], 1.0)
        nc.vector.memset(zero_row[:], 0.0)
        nc.vector.memset(w_scales[:].bitcast(I32), 0)
        nc.vector.memset(bias_row[:], 0.0)
        make_identity(nc, ident_bf[:])
        make_identity(nc, ident_f32[:])

        def load_queries(b):
            nc.sync.dma_start(
                out=q_sb[b][:], in_=q[b].rearrange("(p i) d -> p i d", i=M_TILES)
            )

        def load_keys(b):
            nc.sync.dma_start(out=k_sb[b][:], in_=k[b])

        def load_features(b, g):
            keys = slice(g * K_PASS, (g + 1) * K_PASS)
            nc.sync.dma_start(
                out=f_raw[b, g][:],
                in_=out1[b].rearrange("(p j) n -> p j n", j=PACK)[:, :, keys],
            )

        load_queries(0)
        load_features(0, 0)
        load_keys(0)
        nc.sync.dma_start(
            out=w_codes[:].bitcast(I32),
            in_=wv2_words[0].rearrange("p n t -> p (n t)").bitcast(I32),
        )
        for quad in range(4):
            nc.sync.dma_start(
                out=w_scales[32 * quad : 32 * quad + 4, :].bitcast(I32),
                in_=wv2_scales[0, 4 * quad : 4 * quad + 4, :].bitcast(I32),
            )
        nc.sync.dma_start(out=bias_row[0:1, :], in_=bv2.unsqueeze(0))
        load_features(0, 1)
        load_queries(1)
        load_keys(1)
        load_features(1, 0)
        load_features(1, 1)
        nc.sync.dma_start(out=gamma_bf[:], in_=gamma.partition_broadcast(P))
        for b in range(B):
            nc.sync.dma_start(out=x_sb[b][:], in_=x[b].rearrange("(t p) m -> p t m", p=P))

        qT_ps = {}

        def flip_queries(b):
            qT_ps[b] = ps_flip.tile([P, M_TILES, P], BF16, name="qT_ps", tag="flip")
            for i in range(M_TILES):
                nc.tensor.transpose(qT_ps[b][:, i, :], q_sb[b][:, i, :], ident_bf[:])

        def copy_queries(b):
            edges = (0, P // M_TILES, P) if b == 0 else (0, P)
            for lo, hi in zip(edges[:-1], edges[1:]):
                nc.scalar.copy(
                    out=qT[b][:].rearrange("d (p i) -> d p i", i=M_TILES)[:, lo:hi],
                    in_=qT_ps[b][:].rearrange("d i p -> d p i")[:, lo:hi],
                )

        def group_features(b, g, copy):
            copy(
                out=f_grp[b][:, g].rearrange("p t (c i) j -> p (t c) j i", i=4),
                in_=f_raw[b, g][:].rearrange("p j (c i) -> p c j i", i=4),
            )

        def quantise_features(b, g):
            cols = slice(g * K_PASS, (g + 1) * K_PASS)
            nc.vector.quantize_mx(
                out=f_codes[b][:, cols].bitcast(FP8X4),
                scales=f_scales[b][:, cols],
                in_=f_grp[b][:, g].rearrange("p t r j -> p (t r j)"),
            )

        def spread_bias():
            bias_ps = ps_work.tile([P, C], F32, name="bias_ps", tag="work")
            nc.tensor.matmul(out=bias_ps[:], lhsT=ones_bf[:], rhs=bias_row[:], start=True, stop=True)
            nc.scalar.copy(out=bias_all[:], in_=bias_ps[:])

        val_ps = {}

        def place_of_chunk(v):
            b, rest = divmod(v, CHUNKS)
            g, ct = divmod(rest, C_TILES)
            return b, g, ct

        def multiply_values(v):
            b, g, ct = place_of_chunk(v)
            channels = slice(ct * P, (ct + 1) * P)
            val_ps[v] = ps_work.tile([P, PACK, P], F32, name="val_ps", tag="work")
            for t in range(PACK):
                keys = slice((g * PACK + t) * P, (g * PACK + t + 1) * P)
                nc.tensor.matmul_mx(
                    out=val_ps[v][:, t, :],
                    lhsT=f_codes[b][:, keys].bitcast(FP8X4),
                    lhsT_scale=f_scales[b][:, keys],
                    rhs=w_codes[:, channels].bitcast(FP8X4),
                    rhs_scale=w_scales[:, channels],
                    start=True,
                    stop=True,
                )

        def round_values(v):
            b, g, ct = place_of_chunk(v)
            channels = slice(ct * P, (ct + 1) * P)
            nc.vector.tensor_tensor(
                out=v_grp[b][:, g, channels, :],
                in0=val_ps[v][:].rearrange("p t c -> p c t"),
                in1=bias_all[:, channels].unsqueeze(2).to_broadcast([P, P, PACK]),
                op=ALU.add,
            )

        def quantise_values(b, g):
            nc.vector.quantize_mx(
                out=v_codes[b][:, g, :].bitcast(FP8X4),
                scales=v_scales[b][:, g, :],
                in_=v_grp[b][:, g].rearrange("p c t -> p (c t)"),
            )

        s_ps, bank_max, neg_max, e_sb, e_sums, e_grp, e_codes, e_scales = {}, {}, {}, {}, {}, {}, {}, {}
        eT_ps, total, inv_sum, acc, o_sb, oT_ps = {}, {}, {}, {}, {}, {}

        def scores(i):
            b, mt = divmod(i, M_TILES)
            for g in range(KEY_PASSES):
                s_ps[i, g] = ps_scores.tile([P, BANK], F32, name="s_ps", tag="s_ps%d" % g)
                nc.tensor.matmul(
                    out=s_ps[i, g][:],
                    lhsT=qT[b][:, mt * P : (mt + 1) * P],
                    rhs=k_sb[b][:, g * BANK : (g + 1) * BANK],
                    start=True,
                    stop=True,
                )

        def bank_maxima(i):
            bank_max[i] = stats.tile([P, KEY_PASSES], F32, name="bank_max")
            for g in range(KEY_PASSES):
                nc.vector.reduce_max(
                    out=bank_max[i][:, g : g + 1], in_=s_ps[i, g][:], axis=AXIS_X
                )

        def join_maxima(i):
            neg_max[i] = stats.tile([P, 1], F32, name="neg_max")
            nc.vector.tensor_reduce(
                out=neg_max[i][:], in_=bank_max[i][:], axis=AXIS_X, op=ALU.max, negate=True
            )

        def exponentials(i):
            e_sb[i] = stream.tile([P, N], BF16, name="e_sb")
            e_sums[i] = stats.tile([P, KEY_PASSES], F32, name="e_sums")
            for g in range(KEY_PASSES):
                nc.scalar.activation(
                    out=e_sb[i][:, g * K_PASS : (g + 1) * K_PASS].rearrange(
                        "m (u r e) -> m u r e", u=2, e=2
                    ),
                    in_=s_ps[i, g][:].rearrange("m (u e r) -> m u r e", u=2, e=2),
                    func=ACT.Exp,
                    bias=neg_max[i][:, 0:1],
                    scale=1.0,
                    accum_out=e_sums[i][:, g : g + 1],
                )

        def parts(i):
            return 2 if i == TILES - 1 else 1

        def flip_e(i):
            words = e_sb[i][:].bitcast(F32)
            count = 2 * KEY_PASSES // parts(i)
            for h in range(parts(i)):
                if parts(i) == 1:
                    eT_ps[i, h] = ps_flip.tile([P, count, P], F32, name="eT_ps", tag="flip")
                else:
                    eT_ps[i, h] = ps_scores.tile([P, count, P], F32, name="eT_ps", tag="s_ps%d" % h)
                for w in range(count):
                    first = (h * count + w) * P
                    nc.tensor.transpose(
                        eT_ps[i, h][:, w, :], words[:, first : first + P], ident_f32[:]
                    )

        def gather_e(i, copy=nc.scalar.copy):
            e_grp[i] = stream.tile([P, N], BF16, name="e_grp", align_bytes=64)
            keys = N // parts(i)
            for h in range(parts(i)):
                copy(
                    out=e_grp[i][:, h * keys : (h + 1) * keys]
                    .bitcast(F32)
                    .rearrange("r (g m u) -> r g m u", u=2, m=P),
                    in_=eT_ps[i, h][:].rearrange("r (g u) m -> r g m u", u=2),
                )

        def quantise_e(i):
            e_codes[i] = stream.tile([P, KEY_PASSES * P], U32, name="e_codes", align_bytes=64)
            e_scales[i] = stream.tile([P, KEY_PASSES * P], U8, name="e_scales", align_bytes=64)
            words = KEY_PASSES * P // parts(i)
            for h in range(parts(i)):
                piece = slice(h * words, (h + 1) * words)
                nc.vector.quantize_mx(
                    out=e_codes[i][:, piece].bitcast(FP8X4),
                    scales=e_scales[i][:, piece],
                    in_=e_grp[i][:, h * words * PACK : (h + 1) * words * PACK],
                )

        def add_sums(i):
            total[i] = stats.tile([P, 1], F32, name="total")
            nc.gpsimd.tensor_tensor(
                out=total[i][:], in0=e_sums[i][:, 0:1], in1=e_sums[i][:, 1:2], op=ALU.add
            )

        def invert_sum(i):
            inv_sum[i] = stats.tile([P, 1], F32, name="inv_sum")
            nc.vector.reciprocal(out=inv_sum[i][:], in_=total[i][:])

        def attend(i):
            b = i // M_TILES
            width = C // parts(i)
            for h in range(parts(i)):
                channels = slice(h * width, (h + 1) * width)
                if h == 0:
                    acc[i, h] = ps_work.tile([P, width], F32, name="acc", tag="work")
                else:
                    acc[i, h] = ps_scores.tile([P, width], F32, name="acc", tag="s_ps1")
                for g in range(KEY_PASSES):
                    queries = slice(g * P, (g + 1) * P)
                    nc.tensor.matmul_mx(
                        out=acc[i, h][:],
                        lhsT=e_codes[i][:, queries].bitcast(FP8X4),
                        lhsT_scale=e_scales[i][:, queries],
                        rhs=v_codes[b][:, g, channels].bitcast(FP8X4),
                        rhs_scale=v_scales[b][:, g, channels],
                        start=(g == 0),
                        stop=(g == KEY_PASSES - 1),
                    )

        def times_on_scalar(out, in_, factor):
            nc.scalar.activation(out=out, in_=in_, func=ACT.Copy, scale=factor)

        def times_on_vector(out, in_, factor):
            nc.vector.tensor_scalar(out=out, in0=in_, scalar1=factor, scalar2=None, op0=ALU.mult)

        def normalise(i, times=times_on_scalar):
            width = C // parts(i)
            for h in range(parts(i)):
                o_sb[i, h] = stream.tile([P, width], F32, name="o_sb", tag="o_sb%d" % h)
                times(o_sb[i, h][:], acc[i, h][:], inv_sum[i][:, 0:1])

        def flip_back(i):
            count = C_TILES // parts(i)
            for h in range(parts(i)):
                if h == 0:
                    oT_ps[i, h] = ps_work.tile([P, count, P], F32, name="oT_ps", tag="work")
                else:
                    oT_ps[i, h] = ps_scores.tile([P, count, P], F32, name="oT_ps", tag="s_ps0")
                for ct in range(count):
                    nc.tensor.transpose(
                        oT_ps[i, h][:, ct, :], o_sb[i, h][:, ct * P : (ct + 1) * P], ident_f32[:]
                    )

        def finish(i):
            b, mt = divmod(i, M_TILES)
            queries = slice(mt * P, (mt + 1) * P)
            count = C_TILES // parts(i)
            for h in range(parts(i)):
                cts = slice(h * count, (h + 1) * count)
                result = stream.tile([P, count, P], F32, name="result", bufs=TILES + 1)
                nc.vector.scalar_tensor_tensor(
                    out=result[:],
                    in0=oT_ps[i, h][:],
                    scalar=gamma_f32[:, 0:1],
                    in1=x_sb[b][:, cts, queries],
                    op0=ALU.mult,
                    op1=ALU.add,
                )
                nc.sync.dma_start(
                    out=out[b].rearrange("(t p) m -> p t m", p=P)[:, cts, queries], in_=result[:]
                )

        warm_ps = ps_work.tile([P, BANK], F32, name="warm_ps", tag="work")
        for unused in range(WARM_UPS):
            nc.tensor.matmul(out=warm_ps[:], lhsT=ones_bf[:], rhs=zero_row[:], start=True, stop=True)
        flip_queries(0)
        copy_queries(0)
        group_features(0, 0, nc.vector.tensor_copy)
        nc.gpsimd.tensor_copy(out=gamma_f32[:], in_=gamma_bf[:])

        FIRST_STEP = -1
        LAST = TILES - 1

        def live(i):
            return 0 <= i < TILES

        made = 0
        whole = None
        for step in range(FIRST_STEP, LAST):
            if live(step - 2):
                quantise_e(step - 2)
            due = min(C_TILES if step < FIRST_STEP + 2 else 1, B * CHUNKS - made)
            if due > 0 and made % C_TILES == 0:
                b, g, ct = place_of_chunk(made)
                quantise_features(b, g)
            if live(step + 1):
                scores(step + 1)
                bank_maxima(step + 1)
            if step == FIRST_STEP:
                spread_bias()
                group_features(0, 1, nc.scalar.copy)
            for v in range(made, made + due):
                multiply_values(v)
                if v > made:
                    round_values(v - 1)
            made += due
            if live(step - 4):
                flip_back(step - 4)
            if step in (0, 1):
                group_features(1, step, nc.scalar.copy)
            if live(step - 3):
                normalise(step - 3)
            if step == M_TILES - 3:
                copy_queries(1)
            if whole is not None:
                quantise_values(whole[0], whole[1])
                whole = None
            if due > 0:
                round_values(made - 1)
                if made % C_TILES == 0:
                    whole = place_of_chunk(made - 1)
            if live(step - 1):
                flip_e(step - 1)
                invert_sum(step - 1)
            if live(step - 2):
                attend(step - 2)
            if live(step):
                exponentials(step)
                add_sums(step)
            if live(step + 1):
                join_maxima(step + 1)
            if live(step - 4):
                finish(step - 4)
            if step == M_TILES - 4:
                flip_queries(1)
            if live(step - 1):
                gather_e(step - 1)

        quantise_e(LAST - 2)
        flip_e(LAST - 1)
        flip_back(LAST - 4)
        normalise(LAST - 3)
        exponentials(LAST)
        add_sums(LAST)
        attend(LAST - 2)
        flip_back(LAST - 3)
        invert_sum(LAST - 1)
        gather_e(LAST - 1, nc.vector.tensor_copy)
        flip_e(LAST)
        normalise(LAST - 2)
        finish(LAST - 4)
        gather_e(LAST)
        quantise_e(LAST - 1)
        attend(LAST - 1)
        invert_sum(LAST)
        finish(LAST - 3)
        flip_back(LAST - 2)
        quantise_e(LAST)
        normalise(LAST - 1, times_on_vector)
        attend(LAST)
        normalise(LAST)
        finish(LAST - 2)
        flip_back(LAST - 1)
        flip_back(LAST)
        finish(LAST - 1)
        finish(LAST)
